import numpy as np
import ml_dtypes


def mxq(x, axis, fmt="e4m3"):
    dtype, down = {"e4m3": (ml_dtypes.float8_e4m3fn, 7), "e5m2": (ml_dtypes.float8_e5m2, 14)}[fmt]
    v = np.moveaxis(np.asarray(x, np.float32).astype(ml_dtypes.bfloat16).astype(np.float64), axis, -1)
    blocks = v.reshape(v.shape[:-1] + (-1, 32))
    amax = np.abs(blocks).max(-1, keepdims=True)
    byte = np.maximum(np.where(amax > 0, np.frexp(amax)[1] - 1 + 127, 0) - down, 1)
    scale = np.exp2(byte - 127.0)
    codes = (blocks / scale).astype(np.float32).astype(dtype).astype(np.float64)
    return np.moveaxis((codes * scale).reshape(v.shape), -1, axis)


WIDE = False


def mx_kscale(k):
    if not WIDE:
        return np.ones(k)
    levels = np.array([30, -30])
    if k % 512:
        return np.exp2(np.random.permutation(np.resize(levels, k // 32))).repeat(32)
    a = np.empty((k // 512, 16))
    for p in range(k // 512):
        a[p, :8] = np.random.permutation(np.resize(levels, 8))
        for g in range(8):
            far = levels[np.abs(levels - a[p, g]) >= 10]
            a[p, g + 8] = far[np.random.randint(len(far))]
    return np.exp2(a.ravel()).repeat(32)


BF16 = ml_dtypes.bfloat16


def bf(x):
    return np.asarray(x, np.float32).astype(BF16)


def f64(x):
    return np.asarray(x).astype(np.float64)


B, L, LQ, DM, DH, W = 1, 4096, 1024, 1024, 128, 512
C = L // W


def chunk_banks(x):
    z = np.zeros_like(x[:, :1])
    prev = np.concatenate((z, x[:, :-1]), axis=1)
    nxt = np.concatenate((x[:, 1:], z), axis=1)
    return np.stack((prev, x, nxt), axis=1).sum(axis=2)


def setup_inputs():
    s = mx_kscale(DM)
    return {"kv": bf(np.random.standard_normal((B, L, DM)) * s),
            "Wkv": bf(np.random.standard_normal((DM, 2 * DH)) * 2.0 / np.sqrt(DM * C) / s[:, None])}


def reference(kv, Wkv):
    kvp = mxq(f64(kv), 2, "e5m2") @ mxq(f64(Wkv), 0, "e4m3")
    k, v = kvp[..., :DH], kvp[..., DH:]
    return chunk_banks(k.reshape(B, C, W, DH)), v

@@ -1,0 +1,246 @@
+from contextlib import ExitStack
+
+import concourse.mybir as mybir
+from concourse.masks import make_identity
+
+F32 = mybir.dt.float32
+BF16 = mybir.dt.bfloat16
+U32 = mybir.dt.uint32
+U8 = mybir.dt.uint8
+E5M2X4 = mybir.dt.float8_e5m2_x4
+E4M3X4 = mybir.dt.float8_e4m3fn_x4
+ADD = mybir.AluOpType.add
+
+P = 128
+L, DM, DH, W = 4096, 1024, 128, 512
+CHUNKS = L // W
+PASSES = DM // 512
+LAST = CHUNKS - 1
+PAIRS = 2 * CHUNKS
+
+FLOPS = 2 * L * DM * 2 * DH
+
+RUNS = [[0], [1], [2], [3, 4], [5, 6], [7, 8], [9, 10], [11, 12], [13, 14], [15]]
+UNSPLIT = 2
+FINE = (0, 1, 15)
+V_EMPTIES = ()
+W_AFTER = 1
+VK = 0
+KEYS_FIRST = 1
+V_FINISH = (3, 5, 9, 11, 13)
+
+
+def tile_localxlattention_pa_kernel(tc, kv, Wkv, out_0, out_1):
+    nc = tc.nc
+    kv_v = kv[0].rearrange("(c h p j) k -> h c p j k", h=2, p=P, j=2)
+    v_out = out_1[0].rearrange("(c h p j) n -> h p c j n", h=2, p=P, j=2)
+    k_out = out_0[0].rearrange("b (h p j) n -> h p b j n", h=2, j=2)
+
+    with ExitStack() as ctx:
+        keep = ctx.enter_context(tc.tile_pool(name="keep", bufs=1))
+        ring = ctx.enter_context(tc.tile_pool(name="ring", bufs=6))
+        psum = ctx.enter_context(tc.psum_pool(name="psum", bufs=1))
+        ctx.enter_context(tc.manual_schedule())
+
+        ident = keep.tile([P, P], F32, name="ident")
+        make_identity(nc, ident[:])
+
+        w_raw = keep.tile([P, PASSES, 4, 2 * DH], BF16, name="w_raw", align_bytes=64)
+        w_hbm = Wkv.rearrange("(s p t) n -> p s t n", p=P, t=4)
+        w_grouped = keep.tile([P, PASSES, 2 * DH, 4], BF16, name="w_grouped", align_bytes=64)
+        w_codes = keep.tile([P, PASSES, 2 * DH], U32, name="w_codes", align_bytes=64)
+        w_scales = keep.tile([P, PASSES, 2 * DH], U8, name="w_scales", align_bytes=64)
+
+        raw = [keep.tile([P, 2, DM], BF16, name="raw_%d" % q, align_bytes=64) for q in range(PAIRS)]
+        n_dma = 0
+        for q in range(PAIRS):
+            h, c = divmod(q, CHUNKS)
+            parts = [slice(0, 1), slice(1, 2)] if q == 0 else [slice(0, 2)]
+            for part in parts:
+                if n_dma == W_AFTER:
+                    for s in range(PASSES):
+                        nc.sync.dma_start(out=w_raw[:, s], in_=w_hbm[:, s])
+                n_dma += 1
+                nc.sync.dma_start(out=raw[q][:, part], in_=kv_v[h, c][:, part])
+
+        split = {}
+        grouped = {}
+        codes = {}
+        scales = {}
+        banks = {}
+        accs = {}
+        mids = {}
+        v_sb = [keep.tile([P, CHUNKS + 1, 2, DH], F32, name="v_sb_%d" % h) for h in range(2)]
+        sums = [keep.tile([P, 4, 2, DH], F32, name="sums_%d" % h) for h in range(2)]
+
+        def prepare_w():
+            for s in range(PASSES):
+                nc.vector.tensor_copy(out=w_grouped[:, s], in_=w_raw[:, s].rearrange("p t n -> p n t"))
+
+        def quantize_w():
+            nc.vector.quantize_mx(
+                out=w_codes[:].rearrange("p s n -> p (s n)").bitcast(E4M3X4),
+                scales=w_scales[:].rearrange("p s n -> p (s n)"),
+                in_=w_grouped[:].rearrange("p s n t -> p (s n t)"),
+            )
+
+        def split_words(q):
+            if q < UNSPLIT or q >= PAIRS:
+                return
+            words = raw[q][:].rearrange("p j k -> p (j k)").bitcast(F32)
+            split[q] = ring.tile([P, 2 * PASSES, 2, P], F32, name="split", align_bytes=64)
+            nc.vector.tensor_copy(out=split[q][:], in_=words.rearrange("p (g m u) -> p g u m", m=P, u=2))
+
+        def transposes(q, j):
+            bank = psum.tile([P, PASSES, 2, P], F32, name="bank", bufs=5)
+            banks[(q, j)] = bank
+            for s in range(PASSES):
+                for u in range(2):
+                    if q in split:
+                        src = split[q][:, PASSES * j + s, u, :]
+                    else:
+                        src = raw[q][:, j, :].bitcast(F32)[:, 2 * P * s + u : 2 * P * (s + 1) : 2]
+                    nc.tensor.transpose(bank[:, s, u, :], src, ident[:])
+
+        def empty(q, j):
+            if j == 0:
+                grouped[q] = ring.tile([P, 2, PASSES, P, 2], F32, name="grouped", align_bytes=64)
+            copy = nc.vector.tensor_copy if (q, j) in V_EMPTIES else nc.scalar.copy
+            copy(out=grouped[q][:, j], in_=banks[(q, j)][:].rearrange("p s u r -> p s r u"))
+
+        def quantize(q, j0, n):
+            if j0 == 0:
+                codes[q] = ring.tile([P, 2 * PASSES * P], U32, name="kv_codes", align_bytes=64)
+                scales[q] = ring.tile([P, 2 * PASSES * P], U8, name="kv_scales", align_bytes=64)
+            cols = slice(j0 * PASSES * P, (j0 + n) * PASSES * P)
+            src = grouped[q][:, j0 : j0 + n].rearrange("p j s r u -> p (j s r u)").bitcast(BF16)
+            nc.vector.quantize_mx(out=codes[q][:, cols].bitcast(E5M2X4), scales=scales[q][:, cols], in_=src)
+
+        def quantize_pair(q):
+            if q in FINE:
+                quantize(q, 0, 1)
+                if q == 0:
+                    quantize_w()
+                quantize(q, 1, 1)
+            else:
+                quantize(q, 0, 2)
+
+        def product(q, j, out, n0, n1, first, last):
+            for s in range(PASSES):
+                col = (j * PASSES + s) * P
+                nc.tensor.matmul_mx(
+                    out=out,
+                    lhsT=codes[q][:, col : col + P].bitcast(E5M2X4),
+                    lhsT_scale=scales[q][:, col : col + P],
+                    rhs=w_codes[:, s, n0:n1].bitcast(E4M3X4),
+                    rhs_scale=w_scales[:, s, n0:n1],
+                    start=first and s == 0,
+                    stop=last and s == PASSES - 1,
+                )
+
+        def multiply(q):
+            h, c = divmod(q, CHUNKS)
+            if q == PAIRS - 1:
+                for j in range(2):
+                    accs[(q, j)] = psum.tile([P, DH], F32, name="bank", bufs=5)
+                    product(q, j, accs[(q, j)][:], 0, DH, True, True)
+                accs[q] = psum.tile([P, 2, DH], F32, name="bank", bufs=5)
+                for j in range(2):
+                    product(q, j, accs[q][:, j, :], DH, 2 * DH, True, True)
+            elif c in (0, LAST):
+                accs[q] = psum.tile([P, 2, 2 * DH], F32, name="acc", bufs=2)
+                for j in range(2):
+                    product(q, j, accs[q][:, j, :], 0, 2 * DH, True, True)
+            else:
+                accs[q] = psum.tile([P, 2, DH], F32, name="acc", bufs=2)
+                for j in range(2):
+                    product(q, j, accs[q][:, j, :], DH, 2 * DH, True, True)
+
+        def multiply_keys(q):
+            h, c = divmod(q, CHUNKS)
+            if 0 < c < LAST:
+                if c == 1:
+                    mids[h] = psum.tile([P, 2, DH], F32, name="mid")
+                for j in range(2):
+                    product(q, j, mids[h][:, j, :], 0, DH, c == 1 and j == 0, c == LAST - 1 and j == 1)
+
+        def close_mid(h):
+            nc.scalar.copy(out=sums[h][:, 1], in_=mids[h][:])
+            nc.vector.tensor_tensor(out=sums[h][:, 0], in0=mids[h][:], in1=v_sb[h][:, 0], op=ADD)
+            nc.sync.dma_start(out=k_out[h][:, 0], in_=sums[h][:, 0])
+
+        def finish(q, copy):
+            h, c = divmod(q, CHUNKS)
+            if c == 0:
+                copy(
+                    out=v_sb[h][:, 0:2].rearrange("p w j n -> p j w n"),
+                    in_=accs[q][:].rearrange("p j (w n) -> p j w n", w=2),
+                )
+            elif c < LAST:
+                copy(out=v_sb[h][:, c + 1], in_=accs[q][:])
+            elif h == 0:
+                copy(out=v_sb[h][:, c + 1], in_=accs[q][:, :, DH : 2 * DH])
+                nc.vector.tensor_tensor(
+                    out=sums[h][:, 2:4],
+                    in0=accs[q][:, :, 0:DH].unsqueeze(1).to_broadcast([P, 2, 2, DH]),
+                    in1=sums[h][:, 0:2],
+                    op=ADD,
+                )
+                nc.sync.dma_start(out=k_out[h][:, 1:3], in_=sums[h][:, 2:4])
+            else:
+                for j in range(2):
+                    nc.vector.tensor_tensor(
+                        out=sums[h][:, 2:4, j, :],
+                        in0=accs[(q, j)][:].unsqueeze(1).to_broadcast([P, 2, DH]),
+                        in1=sums[h][:, 0:2, j, :],
+                        op=ADD,
+                    )
+                nc.sync.dma_start(out=k_out[h][:, 1:3], in_=sums[h][:, 2:4])
+                copy(out=v_sb[h][:, c + 1], in_=accs[q][:])
+
+        def store_v(run):
+            h, c0 = divmod(run[0], CHUNKS)
+            c1 = c0 + len(run)
+            nc.sync.dma_start(out=v_out[h][:, c0:c1], in_=v_sb[h][:, c0 + 1 : c1 + 1])
+
+        def turn(run):
+            for q in run:
+                for j in range(2):
+                    transposes(q, j)
+                    empty(q, j)
+
+        turn(RUNS[0])
+        prepare_w()
+        for q in RUNS[1]:
+            split_words(q)
+        for r, run in enumerate(RUNS):
+            ahead = RUNS[r + 1] if r + 1 < len(RUNS) else []
+            if r < len(RUNS) - 1:
+                quantize_pair(run[-1])
+            turn(ahead)
+            for q in RUNS[r + 2] if r + 2 < len(RUNS) else []:
+                split_words(q)
+            for q in ahead if r == len(RUNS) - 2 else ahead[:-1]:
+                quantize_pair(q)
+            closing = run[-1] % CHUNKS == LAST - 1
+            if closing and (KEYS_FIRST == 1 or (KEYS_FIRST == 2 and r > 6)):
+                for q in run:
+                    multiply_keys(q)
+                for q in run:
+                    multiply(q)
+            elif VK:
+                for q in run:
+                    multiply(q)
+                    multiply_keys(q)
+            else:
+                for q in run:
+                    multiply_keys(q)
+                    multiply(q)
+            if closing:
+                close_mid(run[-1] // CHUNKS)
+            for i, q in enumerate(run):
+                finish(q, nc.vector.tensor_copy if q in V_FINISH else nc.scalar.copy)
+                if LAST in run or closing:
+                    store_v([q])
+            if not (LAST in run or closing):
+                store_v(run)

@@ -17,6 +17,7 @@ CHUNKS = L // W
 PASSES = DM // 512
 LAST = CHUNKS - 1
 PAIRS = 2 * CHUNKS
+ORDER = [1, 2, 3, 4, 5, 6, 0, 7]
 
 FLOPS = 2 * L * DM * 2 * DH
 
@@ -25,9 +26,14 @@ UNSPLIT = 2
 FINE = (0, 1, 15)
 V_EMPTIES = ()
 W_AFTER = 1
+VFIRST = 0
+SEP = 1
+FINE_LOAD = 2
+SKIP = {}
+WARM = (0, 0)
 VK = 0
 KEYS_FIRST = 1
-V_FINISH = (3, 5, 9, 11, 13)
+V_FINISH = (3, 5, 9, 11)
 
 
 def tile_localxlattention_pa_kernel(tc, kv, Wkv, out_0, out_1):
@@ -54,8 +60,8 @@ def tile_localxlattention_pa_kernel(tc, kv, Wkv, out_0, out_1):
         raw = [keep.tile([P, 2, DM], BF16, name="raw_%d" % q, align_bytes=64) for q in range(PAIRS)]
         n_dma = 0
         for q in range(PAIRS):
-            h, c = divmod(q, CHUNKS)
-            parts = [slice(0, 1), slice(1, 2)] if q == 0 else [slice(0, 2)]
+            h, c = q // CHUNKS, ORDER[q % CHUNKS]
+            parts = [slice(0, 1), slice(1, 2)] if q < FINE_LOAD else [slice(0, 2)]
             for part in parts:
                 if n_dma == W_AFTER:
                     for s in range(PASSES):
@@ -70,7 +76,7 @@ def tile_localxlattention_pa_kernel(tc, kv, Wkv, out_0, out_1):
         banks = {}
         accs = {}
         mids = {}
-        v_sb = [keep.tile([P, CHUNKS + 1, 2, DH], F32, name="v_sb_%d" % h) for h in range(2)]
+        v_sb = [keep.tile([P, CHUNKS, 2, DH], F32, name="v_sb_%d" % h) for h in range(2)]
         sums = [keep.tile([P, 4, 2, DH], F32, name="sums_%d" % h) for h in range(2)]
 
         def prepare_w():
@@ -89,14 +95,16 @@ def tile_localxlattention_pa_kernel(tc, kv, Wkv, out_0, out_1):
                 return
             words = raw[q][:].rearrange("p j k -> p (j k)").bitcast(F32)
             split[q] = ring.tile([P, 2 * PASSES, 2, P], F32, name="split", align_bytes=64)
-            nc.vector.tensor_copy(out=split[q][:], in_=words.rearrange("p (g m u) -> p g u m", m=P, u=2))
+            g0 = SKIP.get(q, 0)
+            for g in [slice(0, 2), slice(2, 4)] if q < FINE_LOAD and g0 == 0 else [slice(g0, 4)]:
+                nc.vector.tensor_copy(out=split[q][:, g], in_=words.rearrange("p (g m u) -> p g u m", m=P, u=2)[:, g])
 
         def transposes(q, j):
             bank = psum.tile([P, PASSES, 2, P], F32, name="bank", bufs=5)
             banks[(q, j)] = bank
             for s in range(PASSES):
                 for u in range(2):
-                    if q in split:
+                    if q in split and PASSES * j + s >= SKIP.get(q, 0):
                         src = split[q][:, PASSES * j + s, u, :]
                     else:
                         src = raw[q][:, j, :].bitcast(F32)[:, 2 * P * s + u : 2 * P * (s + 1) : 2]
@@ -139,12 +147,12 @@ def tile_localxlattention_pa_kernel(tc, kv, Wkv, out_0, out_1):
                 )
 
         def multiply(q):
-            h, c = divmod(q, CHUNKS)
-            if q == PAIRS - 1:
+            h, c = q // CHUNKS, ORDER[q % CHUNKS]
+            if q >= PAIRS - SEP:
                 for j in range(2):
                     accs[(q, j)] = psum.tile([P, DH], F32, name="bank", bufs=5)
                     product(q, j, accs[(q, j)][:], 0, DH, True, True)
-                accs[q] = psum.tile([P, 2, DH], F32, name="bank", bufs=5)
+                accs[q] = psum.tile([P, 2, DH], F32, name="acc", bufs=2)
                 for j in range(2):
                     product(q, j, accs[q][:, j, :], DH, 2 * DH, True, True)
             elif c in (0, LAST):
@@ -152,42 +160,20 @@ def tile_localxlattention_pa_kernel(tc, kv, Wkv, out_0, out_1):
                 for j in range(2):
                     product(q, j, accs[q][:, j, :], 0, 2 * DH, True, True)
             else:
-                accs[q] = psum.tile([P, 2, DH], F32, name="acc", bufs=2)
-                for j in range(2):
-                    product(q, j, accs[q][:, j, :], DH, 2 * DH, True, True)
-
-        def multiply_keys(q):
-            h, c = divmod(q, CHUNKS)
-            if 0 < c < LAST:
                 if c == 1:
                     mids[h] = psum.tile([P, 2, DH], F32, name="mid")
                 for j in range(2):
                     product(q, j, mids[h][:, j, :], 0, DH, c == 1 and j == 0, c == LAST - 1 and j == 1)
-
-        def close_mid(h):
-            nc.scalar.copy(out=sums[h][:, 1], in_=mids[h][:])
-            nc.vector.tensor_tensor(out=sums[h][:, 0], in0=mids[h][:], in1=v_sb[h][:, 0], op=ADD)
-            nc.sync.dma_start(out=k_out[h][:, 0], in_=sums[h][:, 0])
+                accs[q] = psum.tile([P, 2, DH], F32, name="acc", bufs=2)
+                for j in range(2):
+                    product(q, j, accs[q][:, j, :], DH, 2 * DH, True, True)
 
         def finish(q, copy):
-            h, c = divmod(q, CHUNKS)
-            if c == 0:
-                copy(
-                    out=v_sb[h][:, 0:2].rearrange("p w j n -> p j w n"),
-                    in_=accs[q][:].rearrange("p j (w n) -> p j w n", w=2),
-                )
-            elif c < LAST:
-                copy(out=v_sb[h][:, c + 1], in_=accs[q][:])
-            elif h == 0:
-                copy(out=v_sb[h][:, c + 1], in_=accs[q][:, :, DH : 2 * DH])
-                nc.vector.tensor_tensor(
-                    out=sums[h][:, 2:4],
-                    in0=accs[q][:, :, 0:DH].unsqueeze(1).to_broadcast([P, 2, 2, DH]),
-                    in1=sums[h][:, 0:2],
-                    op=ADD,
-                )
-                nc.sync.dma_start(out=k_out[h][:, 1:3], in_=sums[h][:, 2:4])
-            else:
+            h, c = q // CHUNKS, ORDER[q % CHUNKS]
+            wide = c in (0, LAST) and q < PAIRS - SEP
+            if c == LAST - 1:
+                nc.scalar.copy(out=sums[h][:, 1], in_=mids[h][:])
+            if q == PAIRS - 1:
                 for j in range(2):
                     nc.vector.tensor_tensor(
                         out=sums[h][:, 2:4, j, :],
@@ -196,12 +182,25 @@ def tile_localxlattention_pa_kernel(tc, kv, Wkv, out_0, out_1):
                         op=ADD,
                     )
                 nc.sync.dma_start(out=k_out[h][:, 1:3], in_=sums[h][:, 2:4])
-                copy(out=v_sb[h][:, c + 1], in_=accs[q][:])
+            if c == 0 and (h == 1 or VFIRST):
+                nc.vector.tensor_tensor(out=sums[h][:, 0], in0=accs[q][:, :, 0:DH], in1=sums[h][:, 1], op=ADD)
+                nc.sync.dma_start(out=k_out[h][:, 0], in_=sums[h][:, 0])
+            copy(out=v_sb[h][:, c], in_=accs[q][:, :, DH : 2 * DH] if wide else accs[q][:])
+            if c == 0 and h == 0 and not VFIRST:
+                nc.vector.tensor_tensor(out=sums[h][:, 0], in0=accs[q][:, :, 0:DH], in1=sums[h][:, 1], op=ADD)
+                nc.sync.dma_start(out=k_out[h][:, 0], in_=sums[h][:, 0])
+            elif q == LAST:
+                nc.vector.tensor_tensor(
+                    out=sums[h][:, 2:4],
+                    in0=accs[q][:, :, 0:DH].unsqueeze(1).to_broadcast([P, 2, 2, DH]),
+                    in1=sums[h][:, 0:2],
+                    op=ADD,
+                )
+                nc.sync.dma_start(out=k_out[h][:, 1:3], in_=sums[h][:, 2:4])
 
-        def store_v(run):
-            h, c0 = divmod(run[0], CHUNKS)
-            c1 = c0 + len(run)
-            nc.sync.dma_start(out=v_out[h][:, c0:c1], in_=v_sb[h][:, c0 + 1 : c1 + 1])
+        def store_v(q):
+            h, c = q // CHUNKS, ORDER[q % CHUNKS]
+            nc.sync.dma_start(out=v_out[h][:, c], in_=v_sb[h][:, c])
 
         def turn(run):
             for q in run:
@@ -222,25 +221,8 @@ def tile_localxlattention_pa_kernel(tc, kv, Wkv, out_0, out_1):
                 split_words(q)
             for q in ahead if r == len(RUNS) - 2 else ahead[:-1]:
                 quantize_pair(q)
-            closing = run[-1] % CHUNKS == LAST - 1
-            if closing and (KEYS_FIRST == 1 or (KEYS_FIRST == 2 and r > 6)):
-                for q in run:
-                    multiply_keys(q)
-                for q in run:
-                    multiply(q)
-            elif VK:
-                for q in run:
-                    multiply(q)
-                    multiply_keys(q)
-            else:
-                for q in run:
-                    multiply_keys(q)
-                    multiply(q)
-            if closing:
-                close_mid(run[-1] // CHUNKS)
-            for i, q in enumerate(run):
+            for q in run:
+                multiply(q)
+            for q in run:
                 finish(q, nc.vector.tensor_copy if q in V_FINISH else nc.scalar.copy)
-                if LAST in run or closing:
-                    store_v([q])
-            if not (LAST in run or closing):
-                store_v(run)
+                store_v(q)

@@ -24,8 +24,9 @@ FLOPS = 2 * L * DM * 2 * DH
 RUNS = [[0], [1], [2], [3, 4], [5, 6], [7, 8], [9, 10], [11, 12], [13, 14], [15]]
 UNSPLIT = 2
 FINE = (0, 1, 15)
-V_EMPTIES = ()
+V_EMPTIES = ((15, 1),)
 W_AFTER = 1
+STORES = {6: (0, 7), 7: (7, 8), 10: (1, 4), 12: (4, 6), 13: (6, 7), 14: (0, 1), 15: (7, 8)}
 VFIRST = 0
 SEP = 1
 FINE_LOAD = 2
@@ -33,7 +34,7 @@ SKIP = {}
 WARM = (0, 0)
 VK = 0
 KEYS_FIRST = 1
-V_FINISH = (3, 5, 9, 11)
+V_FINISH = ()
 
 
 def tile_localxlattention_pa_kernel(tc, kv, Wkv, out_0, out_1):
@@ -172,35 +173,36 @@ def tile_localxlattention_pa_kernel(tc, kv, Wkv, out_0, out_1):
             h, c = q // CHUNKS, ORDER[q % CHUNKS]
             wide = c in (0, LAST) and q < PAIRS - SEP
             if c == LAST - 1:
-                nc.scalar.copy(out=sums[h][:, 1], in_=mids[h][:])
+                nc.scalar.copy(out=sums[h][:, 3], in_=mids[h][:])
             if q == PAIRS - 1:
                 for j in range(2):
                     nc.vector.tensor_tensor(
-                        out=sums[h][:, 2:4, j, :],
+                        out=sums[h][:, 1:3, j, :],
                         in0=accs[(q, j)][:].unsqueeze(1).to_broadcast([P, 2, DH]),
-                        in1=sums[h][:, 0:2, j, :],
+                        in1=sums[h][:, 0:4:3, j, :],
                         op=ADD,
                     )
-                nc.sync.dma_start(out=k_out[h][:, 1:3], in_=sums[h][:, 2:4])
+                nc.sync.dma_start(out=k_out[h][:, 1:3], in_=sums[h][:, 1:3])
             if c == 0 and (h == 1 or VFIRST):
-                nc.vector.tensor_tensor(out=sums[h][:, 0], in0=accs[q][:, :, 0:DH], in1=sums[h][:, 1], op=ADD)
+                nc.vector.tensor_tensor(out=sums[h][:, 0], in0=accs[q][:, :, 0:DH], in1=sums[h][:, 3], op=ADD)
                 nc.sync.dma_start(out=k_out[h][:, 0], in_=sums[h][:, 0])
             copy(out=v_sb[h][:, c], in_=accs[q][:, :, DH : 2 * DH] if wide else accs[q][:])
             if c == 0 and h == 0 and not VFIRST:
-                nc.vector.tensor_tensor(out=sums[h][:, 0], in0=accs[q][:, :, 0:DH], in1=sums[h][:, 1], op=ADD)
-                nc.sync.dma_start(out=k_out[h][:, 0], in_=sums[h][:, 0])
+                nc.vector.tensor_tensor(out=sums[h][:, 0], in0=accs[q][:, :, 0:DH], in1=sums[h][:, 3], op=ADD)
             elif q == LAST:
                 nc.vector.tensor_tensor(
-                    out=sums[h][:, 2:4],
+                    out=sums[h][:, 1:3],
                     in0=accs[q][:, :, 0:DH].unsqueeze(1).to_broadcast([P, 2, 2, DH]),
-                    in1=sums[h][:, 0:2],
+                    in1=sums[h][:, 0:4:3],
                     op=ADD,
                 )
-                nc.sync.dma_start(out=k_out[h][:, 1:3], in_=sums[h][:, 2:4])
+                nc.sync.dma_start(out=k_out[h], in_=sums[h][:, 0:3])
 
         def store_v(q):
             h, c = q // CHUNKS, ORDER[q % CHUNKS]
-            nc.sync.dma_start(out=v_out[h][:, c], in_=v_sb[h][:, c])
+            if q in STORES:
+                c0, c1 = STORES[q]
+                nc.sync.dma_start(out=v_out[h][:, c0:c1], in_=v_sb[h][:, c0:c1])
 
         def turn(run):
             for q in run:

from contextlib import ExitStack

import concourse.mybir as mybir
from concourse.masks import make_identity

F32 = mybir.dt.float32
BF16 = mybir.dt.bfloat16
U32 = mybir.dt.uint32
U8 = mybir.dt.uint8
E5M2X4 = mybir.dt.float8_e5m2_x4
E4M3X4 = mybir.dt.float8_e4m3fn_x4
ADD = mybir.AluOpType.add

P = 128
L, DM, DH, W = 4096, 1024, 128, 512
CHUNKS = L // W
PASSES = DM // 512
LAST = CHUNKS - 1
PAIRS = 2 * CHUNKS
ORDER = [1, 2, 3, 4, 5, 6, 0, 7]

FLOPS = 2 * L * DM * 2 * DH

RUNS = [[0], [1], [2], [3, 4], [5, 6], [7, 8], [9, 10], [11, 12], [13, 14], [15]]
UNSPLIT = 2
FINE = (0, 1, 15)
V_EMPTIES = ((15, 1),)
W_AFTER = 1
STORES = {6: (0, 7), 7: (7, 8), 10: (1, 4), 12: (4, 6), 13: (6, 7), 14: (0, 1), 15: (7, 8)}
VFIRST = 0
SEP = 1
FINE_LOAD = 2
SKIP = {}
WARM = (0, 0)
VK = 0
KEYS_FIRST = 1
V_FINISH = ()


def tile_localxlattention_pa_kernel(tc, kv, Wkv, out_0, out_1):
    nc = tc.nc
    kv_v = kv[0].rearrange("(c h p j) k -> h c p j k", h=2, p=P, j=2)
    v_out = out_1[0].rearrange("(c h p j) n -> h p c j n", h=2, p=P, j=2)
    k_out = out_0[0].rearrange("b (h p j) n -> h p b j n", h=2, j=2)

    with ExitStack() as ctx:
        keep = ctx.enter_context(tc.tile_pool(name="keep", bufs=1))
        ring = ctx.enter_context(tc.tile_pool(name="ring", bufs=6))
        psum = ctx.enter_context(tc.psum_pool(name="psum", bufs=1))
        ctx.enter_context(tc.manual_schedule())

        ident = keep.tile([P, P], F32, name="ident")
        make_identity(nc, ident[:])

        w_raw = keep.tile([P, PASSES, 4, 2 * DH], BF16, name="w_raw", align_bytes=64)
        w_hbm = Wkv.rearrange("(s p t) n -> p s t n", p=P, t=4)
        w_grouped = keep.tile([P, PASSES, 2 * DH, 4], BF16, name="w_grouped", align_bytes=64)
        w_codes = keep.tile([P, PASSES, 2 * DH], U32, name="w_codes", align_bytes=64)
        w_scales = keep.tile([P, PASSES, 2 * DH], U8, name="w_scales", align_bytes=64)

        raw = [keep.tile([P, 2, DM], BF16, name="raw_%d" % q, align_bytes=64) for q in range(PAIRS)]
        n_dma = 0
        for q in range(PAIRS):
            h, c = q // CHUNKS, ORDER[q % CHUNKS]
            parts = [slice(0, 1), slice(1, 2)] if q < FINE_LOAD else [slice(0, 2)]
            for part in parts:
                if n_dma == W_AFTER:
                    for s in range(PASSES):
                        nc.sync.dma_start(out=w_raw[:, s], in_=w_hbm[:, s])
                n_dma += 1
                nc.sync.dma_start(out=raw[q][:, part], in_=kv_v[h, c][:, part])

        split = {}
        grouped = {}
        codes = {}
        scales = {}
        banks = {}
        accs = {}
        mids = {}
        v_sb = [keep.tile([P, CHUNKS, 2, DH], F32, name="v_sb_%d" % h) for h in range(2)]
        sums = [keep.tile([P, 4, 2, DH], F32, name="sums_%d" % h) for h in range(2)]

        def prepare_w():
            for s in range(PASSES):
                nc.vector.tensor_copy(out=w_grouped[:, s], in_=w_raw[:, s].rearrange("p t n -> p n t"))

        def quantize_w():
            nc.vector.quantize_mx(
                out=w_codes[:].rearrange("p s n -> p (s n)").bitcast(E4M3X4),
                scales=w_scales[:].rearrange("p s n -> p (s n)"),
                in_=w_grouped[:].rearrange("p s n t -> p (s n t)"),
            )

        def split_words(q):
            if q < UNSPLIT or q >= PAIRS:
                return
            words = raw[q][:].rearrange("p j k -> p (j k)").bitcast(F32)
            split[q] = ring.tile([P, 2 * PASSES, 2, P], F32, name="split", align_bytes=64)
            g0 = SKIP.get(q, 0)
            for g in [slice(0, 2), slice(2, 4)] if q < FINE_LOAD and g0 == 0 else [slice(g0, 4)]:
                nc.vector.tensor_copy(out=split[q][:, g], in_=words.rearrange("p (g m u) -> p g u m", m=P, u=2)[:, g])

        def transposes(q, j):
            bank = psum.tile([P, PASSES, 2, P], F32, name="bank", bufs=5)
            banks[(q, j)] = bank
            for s in range(PASSES):
                for u in range(2):
                    if q in split and PASSES * j + s >= SKIP.get(q, 0):
                        src = split[q][:, PASSES * j + s, u, :]
                    else:
                        src = raw[q][:, j, :].bitcast(F32)[:, 2 * P * s + u : 2 * P * (s + 1) : 2]
                    nc.tensor.transpose(bank[:, s, u, :], src, ident[:])

        def empty(q, j):
            if j == 0:
                grouped[q] = ring.tile([P, 2, PASSES, P, 2], F32, name="grouped", align_bytes=64)
            copy = nc.vector.tensor_copy if (q, j) in V_EMPTIES else nc.scalar.copy
            copy(out=grouped[q][:, j], in_=banks[(q, j)][:].rearrange("p s u r -> p s r u"))

        def quantize(q, j0, n):
            if j0 == 0:
                codes[q] = ring.tile([P, 2 * PASSES * P], U32, name="kv_codes", align_bytes=64)
                scales[q] = ring.tile([P, 2 * PASSES * P], U8, name="kv_scales", align_bytes=64)
            cols = slice(j0 * PASSES * P, (j0 + n) * PASSES * P)
            src = grouped[q][:, j0 : j0 + n].rearrange("p j s r u -> p (j s r u)").bitcast(BF16)
            nc.vector.quantize_mx(out=codes[q][:, cols].bitcast(E5M2X4), scales=scales[q][:, cols], in_=src)

        def quantize_pair(q):
            if q in FINE:
                quantize(q, 0, 1)
                if q == 0:
                    quantize_w()
                quantize(q, 1, 1)
            else:
                quantize(q, 0, 2)

        def product(q, j, out, n0, n1, first, last):
            for s in range(PASSES):
                col = (j * PASSES + s) * P
                nc.tensor.matmul_mx(
                    out=out,
                    lhsT=codes[q][:, col : col + P].bitcast(E5M2X4),
                    lhsT_scale=scales[q][:, col : col + P],
                    rhs=w_codes[:, s, n0:n1].bitcast(E4M3X4),
                    rhs_scale=w_scales[:, s, n0:n1],
                    start=first and s == 0,
                    stop=last and s == PASSES - 1,
                )

        def multiply(q):
            h, c = q // CHUNKS, ORDER[q % CHUNKS]
            if q >= PAIRS - SEP:
                for j in range(2):
                    accs[(q, j)] = psum.tile([P, DH], F32, name="bank", bufs=5)
                    product(q, j, accs[(q, j)][:], 0, DH, True, True)
                accs[q] = psum.tile([P, 2, DH], F32, name="acc", bufs=2)
                for j in range(2):
                    product(q, j, accs[q][:, j, :], DH, 2 * DH, True, True)
            elif c in (0, LAST):
                accs[q] = psum.tile([P, 2, 2 * DH], F32, name="acc", bufs=2)
                for j in range(2):
                    product(q, j, accs[q][:, j, :], 0, 2 * DH, True, True)
            else:
                if c == 1:
                    mids[h] = psum.tile([P, 2, DH], F32, name="mid")
                for j in range(2):
                    product(q, j, mids[h][:, j, :], 0, DH, c == 1 and j == 0, c == LAST - 1 and j == 1)
                accs[q] = psum.tile([P, 2, DH], F32, name="acc", bufs=2)
                for j in range(2):
                    product(q, j, accs[q][:, j, :], DH, 2 * DH, True, True)

        def finish(q, copy):
            h, c = q // CHUNKS, ORDER[q % CHUNKS]
            wide = c in (0, LAST) and q < PAIRS - SEP
            if c == LAST - 1:
                nc.scalar.copy(out=sums[h][:, 3], in_=mids[h][:])
            if q == PAIRS - 1:
                for j in range(2):
                    nc.vector.tensor_tensor(
                        out=sums[h][:, 1:3, j, :],
                        in0=accs[(q, j)][:].unsqueeze(1).to_broadcast([P, 2, DH]),
                        in1=sums[h][:, 0:4:3, j, :],
                        op=ADD,
                    )
                nc.sync.dma_start(out=k_out[h][:, 1:3], in_=sums[h][:, 1:3])
            if c == 0 and (h == 1 or VFIRST):
                nc.vector.tensor_tensor(out=sums[h][:, 0], in0=accs[q][:, :, 0:DH], in1=sums[h][:, 3], op=ADD)
                nc.sync.dma_start(out=k_out[h][:, 0], in_=sums[h][:, 0])
            copy(out=v_sb[h][:, c], in_=accs[q][:, :, DH : 2 * DH] if wide else accs[q][:])
            if c == 0 and h == 0 and not VFIRST:
                nc.vector.tensor_tensor(out=sums[h][:, 0], in0=accs[q][:, :, 0:DH], in1=sums[h][:, 3], op=ADD)
            elif q == LAST:
                nc.vector.tensor_tensor(
                    out=sums[h][:, 1:3],
                    in0=accs[q][:, :, 0:DH].unsqueeze(1).to_broadcast([P, 2, 2, DH]),
                    in1=sums[h][:, 0:4:3],
                    op=ADD,
                )
                nc.sync.dma_start(out=k_out[h], in_=sums[h][:, 0:3])

        def store_v(q):
            h, c = q // CHUNKS, ORDER[q % CHUNKS]
            if q in STORES:
                c0, c1 = STORES[q]
                nc.sync.dma_start(out=v_out[h][:, c0:c1], in_=v_sb[h][:, c0:c1])

        def turn(run):
            for q in run:
                for j in range(2):
                    transposes(q, j)
                    empty(q, j)

        turn(RUNS[0])
        prepare_w()
        for q in RUNS[1]:
            split_words(q)
        for r, run in enumerate(RUNS):
            ahead = RUNS[r + 1] if r + 1 < len(RUNS) else []
            if r < len(RUNS) - 1:
                quantize_pair(run[-1])
            turn(ahead)
            for q in RUNS[r + 2] if r + 2 < len(RUNS) else []:
                split_words(q)
            for q in ahead if r == len(RUNS) - 2 else ahead[:-1]:
                quantize_pair(q)
            for q in run:
                multiply(q)
            for q in run:
                finish(q, nc.vector.tensor_copy if q in V_FINISH else nc.scalar.copy)
                store_v(q)
